import numpy as np
import ml_dtypes


def mxq(x, axis, fmt="e4m3"):
    dtype, down = {"e4m3": (ml_dtypes.float8_e4m3fn, 7), "e5m2": (ml_dtypes.float8_e5m2, 14)}[fmt]
    v = np.moveaxis(np.asarray(x, np.float32).astype(ml_dtypes.bfloat16).astype(np.float64), axis, -1)
    blocks = v.reshape(v.shape[:-1] + (-1, 32))
    amax = np.abs(blocks).max(-1, keepdims=True)
    byte = np.maximum(np.where(amax > 0, np.frexp(amax)[1] - 1 + 127, 0) - down, 1)
    scale = np.exp2(byte - 127.0)
    codes = (blocks / scale).astype(np.float32).astype(dtype).astype(np.float64)
    return np.moveaxis((codes * scale).reshape(v.shape), -1, axis)


WIDE = False


def mx_kscale(k):
    if not WIDE:
        return np.ones(k)
    levels = np.array([10, -10, 5, -5, 0])
    a = np.random.permutation(np.resize(levels, k // 512 * 4)).reshape(k // 512, 4)
    idx = np.arange(k)
    return np.exp2(a[idx // 512, idx % 128 // 32])


BF16 = ml_dtypes.bfloat16


def bf(x):
    return np.asarray(x, np.float32).astype(BF16)


def f64(x):
    return np.asarray(x).astype(np.float64)


N, DK, DV = 4096, 128, 128


def setup_inputs():
    s = mx_kscale(N)
    q = np.random.standard_normal((N, DK)) * 1.4
    k = np.random.standard_normal((N, DK)) * 1.4
    v = np.random.standard_normal((N, DV)) * 2.0
    q[:, 0] = 8.0
    k[:, 0] += np.log(s) * np.sqrt(DK) / 8.0
    v = v * np.mean(s) / s[:, None]
    return {"q": bf(q), "k": bf(k), "v": bf(v)}


def reference(q, k, v):
    scores = f64(q) @ f64(k).T / np.sqrt(DK)
    scores = scores + np.triu(np.ones((N, N)), k=1)
    e = np.exp(scores - scores.max(-1, keepdims=True))
    return (mxq(e, 1, "e4m3") @ mxq(f64(v), 0, "e4m3")) / e.sum(-1, keepdims=True)

@@ -1,0 +1,203 @@
+import math
+from contextlib import ExitStack
+
+import concourse.mybir as mybir
+from concourse.masks import make_identity
+
+F32 = mybir.dt.float32
+BF16 = mybir.dt.bfloat16
+U32 = mybir.dt.uint32
+U8 = mybir.dt.uint8
+FP8X4 = mybir.dt.float8_e4m3fn_x4
+ALU = mybir.AluOpType
+ACT = mybir.ActivationFunctionType
+
+P = 128
+N = 4096
+D = 128
+NT = N // P
+BANK = 512
+NB = N // BANK
+FLOPS = 2 * N * N * (D + D)
+
+ROOT = math.sqrt(128.0)
+SCALE = 1.0 / ROOT
+ROOT_PIECES = (11.3125, 0.0012054443359375, 3.0547380447387695e-06)
+assert abs(sum(ROOT_PIECES) - ROOT) < 1e-10
+
+
+def tile_scaled_dot_product_kernel(tc, q, k, v, out):
+    nc = tc.nc
+    with ExitStack() as ctx:
+        const = ctx.enter_context(tc.tile_pool(name="const", bufs=1))
+        stash_pool = ctx.enter_context(tc.tile_pool(name="stash", bufs=3))
+        e_pool = ctx.enter_context(tc.tile_pool(name="e", bufs=3))
+        work = ctx.enter_context(tc.tile_pool(name="work", bufs=2))
+        small = ctx.enter_context(tc.tile_pool(name="small", bufs=4))
+        ps_s = ctx.enter_context(tc.psum_pool(name="ps_s", bufs=3))
+        ps_t = ctx.enter_context(tc.psum_pool(name="ps_t", bufs=4))
+        ps_o = ctx.enter_context(tc.psum_pool(name="ps_o", bufs=1))
+
+        ident = const.tile([P, P], BF16)
+        make_identity(nc, ident[:])
+        upper = const.tile([P, P], F32)
+        nc.gpsimd.memset(upper[:], 0.0)
+        nc.gpsimd.affine_select(
+            out=upper[:],
+            in_=upper[:],
+            compare_op=ALU.is_ge,
+            fill=1.0,
+            base=0,
+            pattern=[[-1, P]],
+            channel_multiplier=1,
+        )
+        tri = []
+        for i in range(3):
+            m_i = const.tile([P, P], BF16, name="mask%d" % i)
+            nc.vector.tensor_scalar(
+                out=m_i[:], in0=upper[:], scalar1=ROOT_PIECES[i], scalar2=None, op0=ALU.mult
+            )
+            tri.append(m_i)
+
+        q_raw = const.tile([P, NT, D], BF16)
+        k_raw = const.tile([P, NT, D], BF16)
+        v_raw = const.tile([P, NT, D], BF16)
+        q_view = q.rearrange("(j p) d -> p j d", p=P)
+        k_view = k.rearrange("(j p) d -> p j d", p=P)
+        v_view = v.rearrange("(j p) d -> p j d", p=P)
+        nc.sync.dma_start(out=q_raw[:, 0:8, :], in_=q_view[:, 0:8, :])
+        for c in range(4):
+            nc.sync.dma_start(out=k_raw[:, 8 * c : 8 * c + 8, :], in_=k_view[:, 8 * c : 8 * c + 8, :])
+        for c in range(1, 4):
+            nc.sync.dma_start(out=q_raw[:, 8 * c : 8 * c + 8, :], in_=q_view[:, 8 * c : 8 * c + 8, :])
+        nc.sync.dma_start(out=v_raw[:], in_=v_view)
+
+        qT = const.tile([P, N], BF16)
+        kT = const.tile([P, N], BF16)
+
+        def flip(raw, flipped, c, engine_copy):
+            tp = ps_t.tile([P, 8, P], BF16, name="tp")
+            for jj in range(8):
+                nc.tensor.transpose(out=tp[:, jj, :], in_=raw[:, 8 * c + jj, :], identity=ident[:])
+            engine_copy(
+                out=flipped[:, 1024 * c : 1024 * c + 1024], in_=tp[:].rearrange("p a b -> p (a b)")
+            )
+
+        flip(q_raw, qT, 0, nc.scalar.copy)
+        for c in range(4):
+            flip(k_raw, kT, c, nc.vector.tensor_copy if c % 2 == 0 else nc.scalar.copy)
+        for c in range(1, 4):
+            flip(q_raw, qT, c, nc.scalar.copy)
+
+        v_grouped = const.tile([P, N], BF16, align_bytes=64)
+        for h in range(2):
+            nc.gpsimd.tensor_scalar(
+                out=v_grouped[:, 2048 * h : 2048 * h + 2048].rearrange("p (g c t) -> p g c t", g=4, t=4),
+                in0=v_raw[:, 16 * h : 16 * h + 16, :].rearrange("p (g t) c -> p g c t", t=4),
+                scalar1=1.0,
+                scalar2=0.0,
+                op0=ALU.mult,
+                op1=ALU.add,
+            )
+        v_codes = const.tile([P, N // 4], U32, align_bytes=64)
+        v_scales = const.tile([P, N // 4], U8, align_bytes=64)
+        nc.vector.quantize_mx(out=v_codes[:].bitcast(FP8X4), scales=v_scales[:], in_=v_grouped[:])
+
+        for i in range(NT):
+            bd, sd = i // 4, i % 4
+            lo = sd * P
+            lq = qT[:, i * P : (i + 1) * P]
+            stash = stash_pool.tile([P, N], F32)
+            mparts = small.tile([P, 16], F32)
+            n_parts = 0
+            for b in range(NB):
+                s_ps = ps_s.tile([P, BANK], F32)
+                k0 = b * BANK
+                if b != bd:
+                    nc.tensor.matmul(out=s_ps[:], lhsT=lq, rhs=kT[:, k0 : k0 + BANK], start=True, stop=True)
+                else:
+                    if sd > 0:
+                        nc.tensor.matmul(out=s_ps[:, 0:lo], lhsT=lq, rhs=kT[:, k0 : k0 + lo], start=True, stop=True)
+                    nc.tensor.matmul(
+                        out=s_ps[:, lo : lo + P], lhsT=lq, rhs=kT[:, k0 + lo : k0 + lo + P], start=True, stop=False
+                    )
+                    for j in range(3):
+                        nc.tensor.matmul(
+                            out=s_ps[:, lo : lo + P], lhsT=ident[:], rhs=tri[j][:], start=False, stop=(j == 2)
+                        )
+                    if sd < 3:
+                        nc.tensor.matmul(
+                            out=s_ps[:, lo + P : BANK], lhsT=lq, rhs=kT[:, k0 + lo + P : k0 + BANK], start=True, stop=True
+                        )
+                if b < bd:
+                    parts = [(0, BANK, 0.0)]
+                elif b > bd:
+                    parts = [(0, BANK, ROOT)]
+                else:
+                    parts = [(0, lo + P, 0.0)]
+                    if sd < 3:
+                        parts.append((lo + P, BANK, ROOT))
+                for c0, c1, shift in parts:
+                    nc.vector.tensor_scalar(
+                        out=stash[:, k0 + c0 : k0 + c1],
+                        in0=s_ps[:, c0:c1],
+                        scalar1=shift,
+                        scalar2=None,
+                        op0=ALU.add,
+                        op1=ALU.max,
+                        accum_out=mparts[:, n_parts : n_parts + 1],
+                    )
+                    n_parts += 1
+            junk = small.tile([P, 16], F32)
+            nbias = small.tile([P, 1], F32)
+            nc.vector.tensor_scalar(
+                out=junk[:, 0:n_parts],
+                in0=mparts[:, 0:n_parts],
+                scalar1=-SCALE,
+                scalar2=None,
+                op0=ALU.mult,
+                op1=ALU.min,
+                accum_out=nbias[:, 0:1],
+            )
+            e_sb = e_pool.tile([P, N], BF16)
+            rowsum = small.tile([P, 1], F32)
+            nc.scalar.activation(
+                out=e_sb[:], in_=stash[:], func=ACT.Exp, bias=nbias[:, 0:1], scale=SCALE, accum_out=rowsum[:, 0:1]
+            )
+            planes = work.tile([P, N], BF16)
+            for c in range(4):
+                tp = ps_t.tile([P, 8, P], BF16, name="tp")
+                for jj in range(8):
+                    j = 8 * c + jj
+                    nc.tensor.transpose(out=tp[:, jj, :], in_=e_sb[:, j * P : (j + 1) * P], identity=ident[:])
+                nc.scalar.copy(out=planes[:, 1024 * c : 1024 * c + 1024], in_=tp[:].rearrange("p a b -> p (a b)"))
+            grouped = work.tile([P, N], BF16, align_bytes=64)
+            for h in range(2):
+                nc.gpsimd.tensor_scalar(
+                    out=grouped[:, 2048 * h : 2048 * h + 2048].rearrange("p (g c t) -> p g c t", g=4, t=4),
+                    in0=planes[:, 2048 * h : 2048 * h + 2048].rearrange("p (g t c) -> p g c t", g=4, t=4),
+                    scalar1=1.0,
+                    scalar2=0.0,
+                    op0=ALU.mult,
+                    op1=ALU.add,
+                )
+            codes = work.tile([P, N // 4], U32, align_bytes=64)
+            scales = work.tile([P, N // 4], U8, align_bytes=64)
+            nc.vector.quantize_mx(out=codes[:].bitcast(FP8X4), scales=scales[:], in_=grouped[:])
+            acc = ps_o.tile([P, D], F32)
+            for g in range(8):
+                cols = slice(g * P, (g + 1) * P)
+                nc.tensor.matmul_mx(
+                    out=acc[:],
+                    lhsT=codes[:, cols].bitcast(FP8X4),
+                    lhsT_scale=scales[:, cols],
+                    rhs=v_codes[:, cols].bitcast(FP8X4),
+                    rhs_scale=v_scales[:, cols],
+                    start=(g == 0),
+                    stop=(g == 7),
+                )
+            rinv = small.tile([P, 1], F32)
+            nc.vector.reciprocal(out=rinv[:, 0:1], in_=rowsum[:, 0:1])
+            o_sb = small.tile([P, D], F32)
+            nc.vector.tensor_scalar(out=o_sb[:], in0=acc[:], scalar1=rinv[:, 0:1], scalar2=None, op0=ALU.mult)
+            nc.sync.dma_start(out=out[i * P : (i + 1) * P, :], in_=o_sb[:])

@@ -33,10 +33,11 @@ def tile_scaled_dot_product_kernel(tc, q, k, v, out):
         stash_pool = ctx.enter_context(tc.tile_pool(name="stash", bufs=3))
         e_pool = ctx.enter_context(tc.tile_pool(name="e", bufs=3))
         work = ctx.enter_context(tc.tile_pool(name="work", bufs=2))
-        small = ctx.enter_context(tc.tile_pool(name="small", bufs=4))
+        small = ctx.enter_context(tc.tile_pool(name="small", bufs=6))
         ps_s = ctx.enter_context(tc.psum_pool(name="ps_s", bufs=3))
         ps_t = ctx.enter_context(tc.psum_pool(name="ps_t", bufs=4))
         ps_o = ctx.enter_context(tc.psum_pool(name="ps_o", bufs=1))
+        ctx.enter_context(tc.manual_schedule())
 
         ident = const.tile([P, P], BF16)
         make_identity(nc, ident[:])
@@ -53,7 +54,7 @@ def tile_scaled_dot_product_kernel(tc, q, k, v, out):
         )
         tri = []
         for i in range(3):
-            m_i = const.tile([P, P], BF16, name="mask%d" % i)
+            m_i = const.tile([P, P], BF16, name="tri%d" % i)
             nc.vector.tensor_scalar(
                 out=m_i[:], in0=upper[:], scalar1=ROOT_PIECES[i], scalar2=None, op0=ALU.mult
             )
@@ -74,130 +75,185 @@ def tile_scaled_dot_product_kernel(tc, q, k, v, out):
 
         qT = const.tile([P, N], BF16)
         kT = const.tile([P, N], BF16)
+        v_grouped = const.tile([P, N], BF16, align_bytes=64)
+        v_codes = const.tile([P, N // 4], U32, align_bytes=64)
+        v_scales = const.tile([P, N // 4], U8, align_bytes=64)
 
-        def flip(raw, flipped, c, engine_copy):
+        def regroup(dst, src):
+            for h in range(2):
+                nc.gpsimd.tensor_scalar(
+                    out=dst[:, 2048 * h : 2048 * h + 2048].rearrange("p (g c t) -> p g c t", g=4, t=4),
+                    in0=src[:, 2048 * h : 2048 * h + 2048].rearrange("p (g t c) -> p g c t", g=4, t=4),
+                    scalar1=1.0,
+                    scalar2=0.0,
+                    op0=ALU.mult,
+                    op1=ALU.add,
+                )
+
+        def flip_input(raw, flipped, c):
             tp = ps_t.tile([P, 8, P], BF16, name="tp")
             for jj in range(8):
                 nc.tensor.transpose(out=tp[:, jj, :], in_=raw[:, 8 * c + jj, :], identity=ident[:])
-            engine_copy(
-                out=flipped[:, 1024 * c : 1024 * c + 1024], in_=tp[:].rearrange("p a b -> p (a b)")
-            )
+            nc.scalar.copy(out=flipped[:, 1024 * c : 1024 * c + 1024], in_=tp[:].rearrange("p a b -> p (a b)"))
 
-        flip(q_raw, qT, 0, nc.scalar.copy)
-        for c in range(4):
-            flip(k_raw, kT, c, nc.vector.tensor_copy if c % 2 == 0 else nc.scalar.copy)
-        for c in range(1, 4):
-            flip(q_raw, qT, c, nc.scalar.copy)
+        live = {}
 
-        v_grouped = const.tile([P, N], BF16, align_bytes=64)
-        for h in range(2):
-            nc.gpsimd.tensor_scalar(
-                out=v_grouped[:, 2048 * h : 2048 * h + 2048].rearrange("p (g c t) -> p g c t", g=4, t=4),
-                in0=v_raw[:, 16 * h : 16 * h + 16, :].rearrange("p (g t) c -> p g c t", t=4),
-                scalar1=1.0,
-                scalar2=0.0,
-                op0=ALU.mult,
-                op1=ALU.add,
-            )
-        v_codes = const.tile([P, N // 4], U32, align_bytes=64)
-        v_scales = const.tile([P, N // 4], U8, align_bytes=64)
-        nc.vector.quantize_mx(out=v_codes[:].bitcast(FP8X4), scales=v_scales[:], in_=v_grouped[:])
-
-        for i in range(NT):
+        def scores(i, b):
             bd, sd = i // 4, i % 4
             lo = sd * P
+            k0 = b * BANK
             lq = qT[:, i * P : (i + 1) * P]
-            stash = stash_pool.tile([P, N], F32)
-            mparts = small.tile([P, 16], F32)
-            n_parts = 0
-            for b in range(NB):
-                s_ps = ps_s.tile([P, BANK], F32)
-                k0 = b * BANK
-                if b != bd:
-                    nc.tensor.matmul(out=s_ps[:], lhsT=lq, rhs=kT[:, k0 : k0 + BANK], start=True, stop=True)
-                else:
-                    if sd > 0:
-                        nc.tensor.matmul(out=s_ps[:, 0:lo], lhsT=lq, rhs=kT[:, k0 : k0 + lo], start=True, stop=True)
+            if b == 0:
+                live["stash", i] = stash_pool.tile([P, N], F32, name="stash")
+                live["mparts", i] = small.tile([P, 16], F32, name="mparts")
+                live["n", i] = 0
+            stash = live["stash", i]
+            s_ps = ps_s.tile([P, BANK], F32, name="s_ps")
+            if b != bd:
+                nc.tensor.matmul(out=s_ps[:], lhsT=lq, rhs=kT[:, k0 : k0 + BANK], start=True, stop=True)
+            else:
+                if sd > 0:
+                    nc.tensor.matmul(out=s_ps[:, 0:lo], lhsT=lq, rhs=kT[:, k0 : k0 + lo], start=True, stop=True)
+                nc.tensor.matmul(
+                    out=s_ps[:, lo : lo + P], lhsT=lq, rhs=kT[:, k0 + lo : k0 + lo + P], start=True, stop=False
+                )
+                for j in range(3):
                     nc.tensor.matmul(
-                        out=s_ps[:, lo : lo + P], lhsT=lq, rhs=kT[:, k0 + lo : k0 + lo + P], start=True, stop=False
+                        out=s_ps[:, lo : lo + P], lhsT=ident[:], rhs=tri[j][:], start=False, stop=(j == 2)
                     )
-                    for j in range(3):
-                        nc.tensor.matmul(
-                            out=s_ps[:, lo : lo + P], lhsT=ident[:], rhs=tri[j][:], start=False, stop=(j == 2)
-                        )
-                    if sd < 3:
-                        nc.tensor.matmul(
-                            out=s_ps[:, lo + P : BANK], lhsT=lq, rhs=kT[:, k0 + lo + P : k0 + BANK], start=True, stop=True
-                        )
-                if b < bd:
-                    parts = [(0, BANK, 0.0)]
-                elif b > bd:
-                    parts = [(0, BANK, ROOT)]
-                else:
-                    parts = [(0, lo + P, 0.0)]
-                    if sd < 3:
-                        parts.append((lo + P, BANK, ROOT))
-                for c0, c1, shift in parts:
-                    nc.vector.tensor_scalar(
-                        out=stash[:, k0 + c0 : k0 + c1],
-                        in0=s_ps[:, c0:c1],
-                        scalar1=shift,
-                        scalar2=None,
-                        op0=ALU.add,
-                        op1=ALU.max,
-                        accum_out=mparts[:, n_parts : n_parts + 1],
+                if sd < 3:
+                    nc.tensor.matmul(
+                        out=s_ps[:, lo + P : BANK], lhsT=lq, rhs=kT[:, k0 + lo + P : k0 + BANK], start=True, stop=True
                     )
-                    n_parts += 1
-            junk = small.tile([P, 16], F32)
-            nbias = small.tile([P, 1], F32)
+            if b < bd:
+                parts = [(0, BANK, 0.0)]
+            elif b > bd:
+                parts = [(0, BANK, ROOT)]
+            else:
+                parts = [(0, lo + P, 0.0)]
+                if sd < 3:
+                    parts.append((lo + P, BANK, ROOT))
+            for c0, c1, shift in parts:
+                n_parts = live["n", i]
+                nc.vector.tensor_scalar(
+                    out=stash[:, k0 + c0 : k0 + c1],
+                    in0=s_ps[:, c0:c1],
+                    scalar1=shift,
+                    scalar2=None,
+                    op0=ALU.add,
+                    op1=ALU.max,
+                    accum_out=live["mparts", i][:, n_parts : n_parts + 1],
+                )
+                live["n", i] = n_parts + 1
+
+        def row_bias(i):
+            n_parts = live["n", i]
+            junk = small.tile([P, 16], F32, name="junk")
+            nbias = small.tile([P, 1], F32, name="nbias")
             nc.vector.tensor_scalar(
                 out=junk[:, 0:n_parts],
-                in0=mparts[:, 0:n_parts],
+                in0=live["mparts", i][:, 0:n_parts],
                 scalar1=-SCALE,
                 scalar2=None,
                 op0=ALU.mult,
                 op1=ALU.min,
                 accum_out=nbias[:, 0:1],
             )
-            e_sb = e_pool.tile([P, N], BF16)
-            rowsum = small.tile([P, 1], F32)
+            live["nbias", i] = nbias
+
+        def exponentials(i):
+            e_sb = e_pool.tile([P, N], BF16, name="e_sb")
+            rowsum = small.tile([P, 1], F32, name="rowsum")
             nc.scalar.activation(
-                out=e_sb[:], in_=stash[:], func=ACT.Exp, bias=nbias[:, 0:1], scale=SCALE, accum_out=rowsum[:, 0:1]
+                out=e_sb[:],
+                in_=live["stash", i][:],
+                func=ACT.Exp,
+                bias=live["nbias", i][:, 0:1],
+                scale=SCALE,
+                accum_out=rowsum[:, 0:1],
             )
-            planes = work.tile([P, N], BF16)
-            for c in range(4):
-                tp = ps_t.tile([P, 8, P], BF16, name="tp")
-                for jj in range(8):
-                    j = 8 * c + jj
-                    nc.tensor.transpose(out=tp[:, jj, :], in_=e_sb[:, j * P : (j + 1) * P], identity=ident[:])
-                nc.scalar.copy(out=planes[:, 1024 * c : 1024 * c + 1024], in_=tp[:].rearrange("p a b -> p (a b)"))
-            grouped = work.tile([P, N], BF16, align_bytes=64)
-            for h in range(2):
-                nc.gpsimd.tensor_scalar(
-                    out=grouped[:, 2048 * h : 2048 * h + 2048].rearrange("p (g c t) -> p g c t", g=4, t=4),
-                    in0=planes[:, 2048 * h : 2048 * h + 2048].rearrange("p (g t c) -> p g c t", g=4, t=4),
-                    scalar1=1.0,
-                    scalar2=0.0,
-                    op0=ALU.mult,
-                    op1=ALU.add,
+            live["e", i] = e_sb
+            live["rowsum", i] = rowsum
+
+        def flip_e(i, b):
+            if b == 0:
+                live["planes", i] = work.tile([P, N], BF16, name="planes")
+            if b % 2 == 0:
+                live["tp", i] = ps_t.tile([P, 8, P], BF16, name="tp")
+            tp = live["tp", i]
+            for jj in range(4):
+                j = 4 * b + jj
+                nc.tensor.transpose(
+                    out=tp[:, 4 * (b % 2) + jj, :], in_=live["e", i][:, j * P : (j + 1) * P], identity=ident[:]
                 )
-            codes = work.tile([P, N // 4], U32, align_bytes=64)
-            scales = work.tile([P, N // 4], U8, align_bytes=64)
-            nc.vector.quantize_mx(out=codes[:].bitcast(FP8X4), scales=scales[:], in_=grouped[:])
-            acc = ps_o.tile([P, D], F32)
+            if b % 2 == 1:
+                c = b // 2
+                nc.scalar.copy(
+                    out=live["planes", i][:, 1024 * c : 1024 * c + 1024], in_=tp[:].rearrange("p a b -> p (a b)")
+                )
+
+        def regroup_e(i):
+            grouped = work.tile([P, N], BF16, name="grouped", align_bytes=64)
+            regroup(grouped, live["planes", i])
+            live["grouped", i] = grouped
+
+        def quantise_e(i):
+            codes = work.tile([P, N // 4], U32, name="codes", align_bytes=64)
+            scales = work.tile([P, N // 4], U8, name="scales", align_bytes=64)
+            nc.vector.quantize_mx(out=codes[:].bitcast(FP8X4), scales=scales[:], in_=live["grouped", i][:])
+            live["codes", i] = codes
+            live["scales", i] = scales
+
+        def weighted_sum(i):
+            acc = ps_o.tile([P, D], F32, name="acc")
             for g in range(8):
                 cols = slice(g * P, (g + 1) * P)
                 nc.tensor.matmul_mx(
                     out=acc[:],
-                    lhsT=codes[:, cols].bitcast(FP8X4),
-                    lhsT_scale=scales[:, cols],
+                    lhsT=live["codes", i][:, cols].bitcast(FP8X4),
+                    lhsT_scale=live["scales", i][:, cols],
                     rhs=v_codes[:, cols].bitcast(FP8X4),
                     rhs_scale=v_scales[:, cols],
                     start=(g == 0),
                     stop=(g == 7),
                 )
-            rinv = small.tile([P, 1], F32)
-            nc.vector.reciprocal(out=rinv[:, 0:1], in_=rowsum[:, 0:1])
-            o_sb = small.tile([P, D], F32)
-            nc.vector.tensor_scalar(out=o_sb[:], in0=acc[:], scalar1=rinv[:, 0:1], scalar2=None, op0=ALU.mult)
+            live["acc", i] = acc
+
+        def normalise(i):
+            rinv = small.tile([P, 1], F32, name="rinv")
+            nc.vector.reciprocal(out=rinv[:, 0:1], in_=live["rowsum", i][:, 0:1])
+            o_sb = small.tile([P, D], F32, name="o_sb")
+            nc.vector.tensor_scalar(
+                out=o_sb[:], in0=live["acc", i][:], scalar1=rinv[:, 0:1], scalar2=None, op0=ALU.mult
+            )
             nc.sync.dma_start(out=out[i * P : (i + 1) * P, :], in_=o_sb[:])
+
+        def has(i):
+            return 0 <= i < NT
+
+        flip_input(q_raw, qT, 0)
+        regroup(v_grouped, v_raw[:].rearrange("p j d -> p (j d)"))
+        for n in range(NT + 4):
+            if has(n - 3):
+                regroup_e(n - 3)
+            if has(n - 1):
+                exponentials(n - 1)
+            for b in range(NB):
+                if n == 0 and b % 2 == 0:
+                    flip_input(k_raw, kT, b // 2)
+                if n == 1 and b < 3:
+                    flip_input(q_raw, qT, b + 1)
+                if has(n - 2):
+                    flip_e(n - 2, b)
+                if has(n):
+                    scores(n, b)
+                if b == 2 and has(n - 4):
+                    weighted_sum(n - 4)
+            if has(n):
+                row_bias(n)
+            if n == 1:
+                nc.vector.quantize_mx(out=v_codes[:].bitcast(FP8X4), scales=v_scales[:], in_=v_grouped[:])
+            if has(n - 3):
+                quantise_e(n - 3)
+            if has(n - 4):
+                normalise(n - 4)

@@ -189,7 +189,8 @@ def tile_scaled_dot_product_kernel(tc, q, k, v, out):
             if b % 2 == 1:
                 c = b // 2
                 nc.scalar.copy(
-                    out=live["planes", i][:, 1024 * c : 1024 * c + 1024], in_=tp[:].rearrange("p a b -> p (a b)")
+                    out=live["planes", i][:, 1024 * c : 1024 * c + 1024].bitcast(F32),
+                    in_=tp[:].rearrange("p a b -> p (a b)").bitcast(F32),
                 )
 
         def regroup_e(i):

@@ -41,6 +41,8 @@ def tile_scaled_dot_product_kernel(tc, q, k, v, out):
 
         ident = const.tile([P, P], BF16)
         make_identity(nc, ident[:])
+        ident_f = const.tile([P, P], F32)
+        make_identity(nc, ident_f[:])
         upper = const.tile([P, P], F32)
         nc.gpsimd.memset(upper[:], 0.0)
         nc.gpsimd.affine_select(
@@ -65,13 +67,13 @@ def tile_scaled_dot_product_kernel(tc, q, k, v, out):
         v_raw = const.tile([P, NT, D], BF16)
         q_view = q.rearrange("(j p) d -> p j d", p=P)
         k_view = k.rearrange("(j p) d -> p j d", p=P)
-        v_view = v.rearrange("(j p) d -> p j d", p=P)
+        v_view = v.rearrange("(a p e) d -> p a (e d)", p=P, e=2)
         nc.sync.dma_start(out=q_raw[:, 0:8, :], in_=q_view[:, 0:8, :])
         for c in range(4):
             nc.sync.dma_start(out=k_raw[:, 8 * c : 8 * c + 8, :], in_=k_view[:, 8 * c : 8 * c + 8, :])
         for c in range(1, 4):
             nc.sync.dma_start(out=q_raw[:, 8 * c : 8 * c + 8, :], in_=q_view[:, 8 * c : 8 * c + 8, :])
-        nc.sync.dma_start(out=v_raw[:], in_=v_view)
+        nc.sync.dma_start(out=v_raw[:].rearrange("p (a e) d -> p a (e d)", e=2), in_=v_view)
 
         qT = const.tile([P, N], BF16)
         kT = const.tile([P, N], BF16)
@@ -91,7 +93,7 @@ def tile_scaled_dot_product_kernel(tc, q, k, v, out):
                 )
 
         def flip_input(raw, flipped, c):
-            tp = ps_t.tile([P, 8, P], BF16, name="tp")
+            tp = ps_t.tile([P, 8, P], BF16, name="tp_in", tag="tp")
             for jj in range(8):
                 nc.tensor.transpose(out=tp[:, jj, :], in_=raw[:, 8 * c + jj, :], identity=ident[:])
             nc.scalar.copy(out=flipped[:, 1024 * c : 1024 * c + 1024], in_=tp[:].rearrange("p a b -> p (a b)"))
@@ -175,28 +177,26 @@ def tile_scaled_dot_product_kernel(tc, q, k, v, out):
             live["e", i] = e_sb
             live["rowsum", i] = rowsum
 
-        def flip_e(i, b):
-            if b == 0:
-                live["planes", i] = work.tile([P, N], BF16, name="planes")
-            if b % 2 == 0:
-                live["tp", i] = ps_t.tile([P, 8, P], BF16, name="tp")
+        def flip_e(i, g):
+            if g == 0:
+                live["grouped", i] = work.tile([P, N], BF16, name="grouped", align_bytes=64)
+            if g % 2 == 0:
+                live["tp", i] = ps_t.tile([P, 4, P], F32, name="tp_e", tag="tp")
             tp = live["tp", i]
-            for jj in range(4):
-                j = 4 * b + jj
+            words = live["e", i][:].bitcast(F32)
+            for u in range(2):
+                w = 2 * g + u
                 nc.tensor.transpose(
-                    out=tp[:, 4 * (b % 2) + jj, :], in_=live["e", i][:, j * P : (j + 1) * P], identity=ident[:]
+                    out=tp[:, 2 * (g % 2) + u, :], in_=words[:, w * P : (w + 1) * P], identity=ident_f[:]
                 )
-            if b % 2 == 1:
-                c = b // 2
+            if g % 2 == 1:
+                c = g // 2
                 nc.scalar.copy(
-                    out=live["planes", i][:, 1024 * c : 1024 * c + 1024].bitcast(F32),
-                    in_=tp[:].rearrange("p a b -> p (a b)").bitcast(F32),
+                    out=live["grouped", i][:]
+                    .bitcast(F32)[:, 512 * c : 512 * c + 512]
+                    .rearrange("p (g c u) -> p g c u", g=2, u=2),
+                    in_=tp[:].rearrange("p (g u) c -> p g c u", u=2),
                 )
-
-        def regroup_e(i):
-            grouped = work.tile([P, N], BF16, name="grouped", align_bytes=64)
-            regroup(grouped, live["planes", i])
-            live["grouped", i] = grouped
 
         def quantise_e(i):
             codes = work.tile([P, N // 4], U32, name="codes", align_bytes=64)
@@ -234,11 +234,11 @@ def tile_scaled_dot_product_kernel(tc, q, k, v, out):
 
         flip_input(q_raw, qT, 0)
         regroup(v_grouped, v_raw[:].rearrange("p j d -> p (j d)"))
-        for n in range(NT + 4):
-            if has(n - 3):
-                regroup_e(n - 3)
+        for n in range(NT + 3):
             if has(n - 1):
                 exponentials(n - 1)
+            if has(n - 3):
+                quantise_e(n - 3)
             for b in range(NB):
                 if n == 0 and b % 2 == 0:
                     flip_input(k_raw, kT, b // 2)
@@ -248,13 +248,11 @@ def tile_scaled_dot_product_kernel(tc, q, k, v, out):
                     flip_e(n - 2, b)
                 if has(n):
                     scores(n, b)
-                if b == 2 and has(n - 4):
-                    weighted_sum(n - 4)
+                if b == 2 and has(n - 3):
+                    weighted_sum(n - 3)
             if has(n):
                 row_bias(n)
             if n == 1:
                 nc.vector.quantize_mx(out=v_codes[:].bitcast(FP8X4), scales=v_scales[:], in_=v_grouped[:])
             if has(n - 3):
-                quantise_e(n - 3)
-            if has(n - 4):
-                normalise(n - 4)
+                normalise(n - 3)

@@ -24,6 +24,7 @@ ROOT = math.sqrt(128.0)
 SCALE = 1.0 / ROOT
 ROOT_PIECES = (11.3125, 0.0012054443359375, 3.0547380447387695e-06)
 assert abs(sum(ROOT_PIECES) - ROOT) < 1e-10
+Q_REST = ((1, 8), (8, 16), (16, 24), (24, 32))
 
 
 def tile_scaled_dot_product_kernel(tc, q, k, v, out):
@@ -68,11 +69,11 @@ def tile_scaled_dot_product_kernel(tc, q, k, v, out):
         q_view = q.rearrange("(j p) d -> p j d", p=P)
         k_view = k.rearrange("(j p) d -> p j d", p=P)
         v_view = v.rearrange("(a p e) d -> p a (e d)", p=P, e=2)
-        nc.sync.dma_start(out=q_raw[:, 0:8, :], in_=q_view[:, 0:8, :])
-        for c in range(4):
-            nc.sync.dma_start(out=k_raw[:, 8 * c : 8 * c + 8, :], in_=k_view[:, 8 * c : 8 * c + 8, :])
-        for c in range(1, 4):
-            nc.sync.dma_start(out=q_raw[:, 8 * c : 8 * c + 8, :], in_=q_view[:, 8 * c : 8 * c + 8, :])
+        nc.sync.dma_start(out=q_raw[:, 0:1, :], in_=q_view[:, 0:1, :])
+        for b in range(NB):
+            nc.sync.dma_start(out=k_raw[:, 4 * b : 4 * b + 4, :], in_=k_view[:, 4 * b : 4 * b + 4, :])
+        for j0, j1 in Q_REST:
+            nc.sync.dma_start(out=q_raw[:, j0:j1, :], in_=q_view[:, j0:j1, :])
         nc.sync.dma_start(out=v_raw[:].rearrange("p (a e) d -> p a (e d)", e=2), in_=v_view)
 
         qT = const.tile([P, N], BF16)
@@ -92,11 +93,13 @@ def tile_scaled_dot_product_kernel(tc, q, k, v, out):
                     op1=ALU.add,
                 )
 
-        def flip_input(raw, flipped, c):
+        def flip_input(raw, flipped, j0, j1):
             tp = ps_t.tile([P, 8, P], BF16, name="tp_in", tag="tp")
-            for jj in range(8):
-                nc.tensor.transpose(out=tp[:, jj, :], in_=raw[:, 8 * c + jj, :], identity=ident[:])
-            nc.scalar.copy(out=flipped[:, 1024 * c : 1024 * c + 1024], in_=tp[:].rearrange("p a b -> p (a b)"))
+            for j in range(j0, j1):
+                nc.tensor.transpose(out=tp[:, j - j0, :], in_=raw[:, j, :], identity=ident[:])
+            nc.scalar.copy(
+                out=flipped[:, j0 * P : j1 * P], in_=tp[:, 0 : j1 - j0, :].rearrange("p a b -> p (a b)")
+            )
 
         live = {}
 
@@ -191,7 +194,9 @@ def tile_scaled_dot_product_kernel(tc, q, k, v, out):
                 )
             if g % 2 == 1:
                 c = g // 2
-                nc.scalar.copy(
+                by_vector = i == NT - 2 or (i == NT - 1 and c % 2 == 1)
+                copy = nc.vector.tensor_copy if by_vector else nc.scalar.copy
+                copy(
                     out=live["grouped", i][:]
                     .bitcast(F32)[:, 512 * c : 512 * c + 512]
                     .rearrange("p (g c u) -> p g c u", g=2, u=2),
@@ -202,8 +207,11 @@ def tile_scaled_dot_product_kernel(tc, q, k, v, out):
             codes = work.tile([P, N // 4], U32, name="codes", align_bytes=64)
             scales = work.tile([P, N // 4], U8, name="scales", align_bytes=64)
             nc.vector.quantize_mx(out=codes[:].bitcast(FP8X4), scales=scales[:], in_=live["grouped", i][:])
+            rinv = small.tile([P, 1], F32, name="rinv")
+            nc.vector.reciprocal(out=rinv[:, 0:1], in_=live["rowsum", i][:, 0:1])
             live["codes", i] = codes
             live["scales", i] = scales
+            live["rinv", i] = rinv
 
         def weighted_sum(i):
             acc = ps_o.tile([P, D], F32, name="acc")
@@ -221,18 +229,14 @@ def tile_scaled_dot_product_kernel(tc, q, k, v, out):
             live["acc", i] = acc
 
         def normalise(i):
-            rinv = small.tile([P, 1], F32, name="rinv")
-            nc.vector.reciprocal(out=rinv[:, 0:1], in_=live["rowsum", i][:, 0:1])
             o_sb = small.tile([P, D], F32, name="o_sb")
-            nc.vector.tensor_scalar(
-                out=o_sb[:], in0=live["acc", i][:], scalar1=rinv[:, 0:1], scalar2=None, op0=ALU.mult
-            )
+            nc.scalar.activation(out=o_sb[:], in_=live["acc", i][:], func=ACT.Copy, scale=live["rinv", i][:, 0:1])
             nc.sync.dma_start(out=out[i * P : (i + 1) * P, :], in_=o_sb[:])
 
         def has(i):
             return 0 <= i < NT
 
-        flip_input(q_raw, qT, 0)
+        flip_input(q_raw, qT, 0, 1)
         regroup(v_grouped, v_raw[:].rearrange("p j d -> p (j d)"))
         for n in range(NT + 3):
             if has(n - 1):
@@ -240,10 +244,10 @@ def tile_scaled_dot_product_kernel(tc, q, k, v, out):
             if has(n - 3):
                 quantise_e(n - 3)
             for b in range(NB):
-                if n == 0 and b % 2 == 0:
-                    flip_input(k_raw, kT, b // 2)
+                if n == 0:
+                    flip_input(k_raw, kT, 4 * b, 4 * b + 4)
                 if n == 1 and b < 3:
-                    flip_input(q_raw, qT, b + 1)
+                    flip_input(q_raw, qT, Q_REST[b + 1][0], Q_REST[b + 1][1])
                 if has(n - 2):
                     flip_e(n - 2, b)
                 if has(n):
@@ -252,6 +256,8 @@ def tile_scaled_dot_product_kernel(tc, q, k, v, out):
                     weighted_sum(n - 3)
             if has(n):
                 row_bias(n)
+            if n == 0:
+                flip_input(q_raw, qT, Q_REST[0][0], Q_REST[0][1])
             if n == 1:
                 nc.vector.quantize_mx(out=v_codes[:].bitcast(FP8X4), scales=v_scales[:], in_=v_grouped[:])
             if has(n - 3):

@@ -35,8 +35,8 @@ def tile_scaled_dot_product_kernel(tc, q, k, v, out):
         e_pool = ctx.enter_context(tc.tile_pool(name="e", bufs=3))
         work = ctx.enter_context(tc.tile_pool(name="work", bufs=2))
         small = ctx.enter_context(tc.tile_pool(name="small", bufs=6))
-        ps_s = ctx.enter_context(tc.psum_pool(name="ps_s", bufs=3))
-        ps_t = ctx.enter_context(tc.psum_pool(name="ps_t", bufs=4))
+        ps_s = ctx.enter_context(tc.psum_pool(name="ps_s", bufs=4))
+        ps_t = ctx.enter_context(tc.psum_pool(name="ps_t", bufs=3))
         ps_o = ctx.enter_context(tc.psum_pool(name="ps_o", bufs=1))
         ctx.enter_context(tc.manual_schedule())
 
@@ -180,28 +180,23 @@ def tile_scaled_dot_product_kernel(tc, q, k, v, out):
             live["e", i] = e_sb
             live["rowsum", i] = rowsum
 
-        def flip_e(i, g):
-            if g == 0:
+        def flip_e(i, c):
+            if c == 0:
                 live["grouped", i] = work.tile([P, N], BF16, name="grouped", align_bytes=64)
-            if g % 2 == 0:
-                live["tp", i] = ps_t.tile([P, 4, P], F32, name="tp_e", tag="tp")
-            tp = live["tp", i]
+            tp = ps_t.tile([P, 4, P], F32, name="tp_e", tag="tp")
             words = live["e", i][:].bitcast(F32)
-            for u in range(2):
-                w = 2 * g + u
+            for w in range(4):
                 nc.tensor.transpose(
-                    out=tp[:, 2 * (g % 2) + u, :], in_=words[:, w * P : (w + 1) * P], identity=ident_f[:]
+                    out=tp[:, w, :], in_=words[:, (4 * c + w) * P : (4 * c + w + 1) * P], identity=ident_f[:]
                 )
-            if g % 2 == 1:
-                c = g // 2
-                by_vector = i == NT - 2 or (i == NT - 1 and c % 2 == 1)
-                copy = nc.vector.tensor_copy if by_vector else nc.scalar.copy
-                copy(
-                    out=live["grouped", i][:]
-                    .bitcast(F32)[:, 512 * c : 512 * c + 512]
-                    .rearrange("p (g c u) -> p g c u", g=2, u=2),
-                    in_=tp[:].rearrange("p (g u) c -> p g c u", u=2),
-                )
+            by_vector = i == NT - 2 or (i == NT - 1 and c % 2 == 1)
+            copy = nc.vector.tensor_copy if by_vector else nc.scalar.copy
+            copy(
+                out=live["grouped", i][:]
+                .bitcast(F32)[:, 512 * c : 512 * c + 512]
+                .rearrange("p (g c u) -> p g c u", g=2, u=2),
+                in_=tp[:].rearrange("p (g u) c -> p g c u", u=2),
+            )
 
         def quantise_e(i):
             codes = work.tile([P, N // 4], U32, name="codes", align_bytes=64)
@@ -213,12 +208,13 @@ def tile_scaled_dot_product_kernel(tc, q, k, v, out):
             live["scales", i] = scales
             live["rinv", i] = rinv
 
-        def weighted_sum(i):
-            acc = ps_o.tile([P, D], F32, name="acc")
-            for g in range(8):
+        def weighted_sum(i, g0, g1):
+            if g0 == 0:
+                live["acc", i] = ps_o.tile([P, D], F32, name="acc")
+            for g in range(g0, g1):
                 cols = slice(g * P, (g + 1) * P)
                 nc.tensor.matmul_mx(
-                    out=acc[:],
+                    out=live["acc", i][:],
                     lhsT=live["codes", i][:, cols].bitcast(FP8X4),
                     lhsT_scale=live["scales", i][:, cols],
                     rhs=v_codes[:, cols].bitcast(FP8X4),
@@ -226,7 +222,6 @@ def tile_scaled_dot_product_kernel(tc, q, k, v, out):
                     start=(g == 0),
                     stop=(g == 7),
                 )
-            live["acc", i] = acc
 
         def normalise(i):
             o_sb = small.tile([P, D], F32, name="o_sb")
@@ -248,12 +243,14 @@ def tile_scaled_dot_product_kernel(tc, q, k, v, out):
                     flip_input(k_raw, kT, 4 * b, 4 * b + 4)
                 if n == 1 and b < 3:
                     flip_input(q_raw, qT, Q_REST[b + 1][0], Q_REST[b + 1][1])
-                if has(n - 2):
-                    flip_e(n - 2, b)
+                if has(n - 2) and 1 <= b <= 3:
+                    flip_e(n - 2, b - 1)
+                if has(n - 3) and 4 <= b <= 6:
+                    weighted_sum(n - 3, 3 * (b - 4), min(3 * (b - 4) + 3, 8))
                 if has(n):
                     scores(n, b)
-                if b == 2 and has(n - 3):
-                    weighted_sum(n - 3)
+            if has(n - 2):
+                flip_e(n - 2, 3)
             if has(n):
                 row_bias(n)
             if n == 0:

@@ -33,6 +33,7 @@ def tile_scaled_dot_product_kernel(tc, q, k, v, out):
         const = ctx.enter_context(tc.tile_pool(name="const", bufs=1))
         stash_pool = ctx.enter_context(tc.tile_pool(name="stash", bufs=3))
         e_pool = ctx.enter_context(tc.tile_pool(name="e", bufs=3))
+        grouped_pool = ctx.enter_context(tc.tile_pool(name="grouped", bufs=3))
         work = ctx.enter_context(tc.tile_pool(name="work", bufs=2))
         small = ctx.enter_context(tc.tile_pool(name="small", bufs=6))
         ps_s = ctx.enter_context(tc.psum_pool(name="ps_s", bufs=4))
@@ -182,15 +183,14 @@ def tile_scaled_dot_product_kernel(tc, q, k, v, out):
 
         def flip_e(i, c):
             if c == 0:
-                live["grouped", i] = work.tile([P, N], BF16, name="grouped", align_bytes=64)
+                live["grouped", i] = grouped_pool.tile([P, N], BF16, name="grouped", align_bytes=64)
             tp = ps_t.tile([P, 4, P], F32, name="tp_e", tag="tp")
             words = live["e", i][:].bitcast(F32)
             for w in range(4):
                 nc.tensor.transpose(
                     out=tp[:, w, :], in_=words[:, (4 * c + w) * P : (4 * c + w + 1) * P], identity=ident_f[:]
                 )
-            by_vector = i == NT - 2 or (i == NT - 1 and c % 2 == 1)
-            copy = nc.vector.tensor_copy if by_vector else nc.scalar.copy
+            copy = nc.vector.tensor_copy if i == NT - 2 else nc.scalar.copy
             copy(
                 out=live["grouped", i][:]
                 .bitcast(F32)[:, 512 * c : 512 * c + 512]
@@ -233,11 +233,11 @@ def tile_scaled_dot_product_kernel(tc, q, k, v, out):
 
         flip_input(q_raw, qT, 0, 1)
         regroup(v_grouped, v_raw[:].rearrange("p j d -> p (j d)"))
-        for n in range(NT + 3):
+        for n in range(NT + 4):
             if has(n - 1):
                 exponentials(n - 1)
-            if has(n - 3):
-                quantise_e(n - 3)
+            if has(n - 4):
+                quantise_e(n - 4)
             for b in range(NB):
                 if n == 0:
                     flip_input(k_raw, kT, 4 * b, 4 * b + 4)
@@ -245,10 +245,12 @@ def tile_scaled_dot_product_kernel(tc, q, k, v, out):
                     flip_input(q_raw, qT, Q_REST[b + 1][0], Q_REST[b + 1][1])
                 if has(n - 2) and 1 <= b <= 3:
                     flip_e(n - 2, b - 1)
-                if has(n - 3) and 4 <= b <= 6:
-                    weighted_sum(n - 3, 3 * (b - 4), min(3 * (b - 4) + 3, 8))
+                if has(n - 4) and 4 <= b <= 6:
+                    weighted_sum(n - 4, 3 * (b - 4), min(3 * (b - 4) + 3, 8))
                 if has(n):
                     scores(n, b)
+            if has(n - 4):
+                normalise(n - 4)
             if has(n - 2):
                 flip_e(n - 2, 3)
             if has(n):
@@ -257,5 +259,3 @@ def tile_scaled_dot_product_kernel(tc, q, k, v, out):
                 flip_input(q_raw, qT, Q_REST[0][0], Q_REST[0][1])
             if n == 1:
                 nc.vector.quantize_mx(out=v_codes[:].bitcast(FP8X4), scales=v_scales[:], in_=v_grouped[:])
-            if has(n - 3):
-                normalise(n - 3)

@@ -14,16 +14,12 @@ ACT = mybir.ActivationFunctionType
 
 P = 128
 N = 4096
-D = 128
-NT = N // P
+TILES = N // P
 BANK = 512
-NB = N // BANK
-FLOPS = 2 * N * N * (D + D)
+BANKS = N // BANK
+FLOPS = 2 * N * N * (P + P)
 
 ROOT = math.sqrt(128.0)
-SCALE = 1.0 / ROOT
-ROOT_PIECES = (11.3125, 0.0012054443359375, 3.0547380447387695e-06)
-assert abs(sum(ROOT_PIECES) - ROOT) < 1e-10
 Q_REST = ((1, 8), (8, 16), (16, 24), (24, 32))
 
 
@@ -34,219 +30,193 @@ def tile_scaled_dot_product_kernel(tc, q, k, v, out):
         stash_pool = ctx.enter_context(tc.tile_pool(name="stash", bufs=3))
         e_pool = ctx.enter_context(tc.tile_pool(name="e", bufs=3))
         grouped_pool = ctx.enter_context(tc.tile_pool(name="grouped", bufs=3))
-        work = ctx.enter_context(tc.tile_pool(name="work", bufs=2))
+        codes_pool = ctx.enter_context(tc.tile_pool(name="codes", bufs=2))
         small = ctx.enter_context(tc.tile_pool(name="small", bufs=6))
-        ps_s = ctx.enter_context(tc.psum_pool(name="ps_s", bufs=4))
-        ps_t = ctx.enter_context(tc.psum_pool(name="ps_t", bufs=3))
-        ps_o = ctx.enter_context(tc.psum_pool(name="ps_o", bufs=1))
+        ps_scores = ctx.enter_context(tc.psum_pool(name="ps_scores", bufs=4))
+        ps_flip = ctx.enter_context(tc.psum_pool(name="ps_flip", bufs=3))
+        ps_out = ctx.enter_context(tc.psum_pool(name="ps_out", bufs=1))
         ctx.enter_context(tc.manual_schedule())
 
         ident = const.tile([P, P], BF16)
         make_identity(nc, ident[:])
         ident_f = const.tile([P, P], F32)
         make_identity(nc, ident_f[:])
-        upper = const.tile([P, P], F32)
-        nc.gpsimd.memset(upper[:], 0.0)
+        below = const.tile([P, P], F32)
+        nc.gpsimd.memset(below[:], 0.0)
         nc.gpsimd.affine_select(
-            out=upper[:],
-            in_=upper[:],
+            out=below[:],
+            in_=below[:],
             compare_op=ALU.is_ge,
             fill=1.0,
             base=0,
-            pattern=[[-1, P]],
-            channel_multiplier=1,
+            pattern=[[1, P]],
+            channel_multiplier=-1,
         )
-        tri = []
-        for i in range(3):
-            m_i = const.tile([P, P], BF16, name="tri%d" % i)
-            nc.vector.tensor_scalar(
-                out=m_i[:], in0=upper[:], scalar1=ROOT_PIECES[i], scalar2=None, op0=ALU.mult
-            )
-            tri.append(m_i)
+        ones = const.tile([P, P], F32)
+        nc.gpsimd.memset(ones[:], 1.0)
+        add_diagonal = const.tile([P, P], F32)
+        nc.vector.tensor_scalar(out=add_diagonal[:], in0=below[:], scalar1=ROOT, scalar2=None, op0=ALU.mult)
+        add_right = const.tile([P, P], F32)
+        nc.vector.tensor_scalar(out=add_right[:], in0=ones[:], scalar1=ROOT, scalar2=None, op0=ALU.mult)
 
-        q_raw = const.tile([P, NT, D], BF16)
-        k_raw = const.tile([P, NT, D], BF16)
-        v_raw = const.tile([P, NT, D], BF16)
+        q_raw = const.tile([P, TILES, P], BF16)
+        k_raw = const.tile([P, TILES, P], BF16)
         q_view = q.rearrange("(j p) d -> p j d", p=P)
         k_view = k.rearrange("(j p) d -> p j d", p=P)
-        v_view = v.rearrange("(a p e) d -> p a (e d)", p=P, e=2)
         nc.sync.dma_start(out=q_raw[:, 0:1, :], in_=q_view[:, 0:1, :])
-        for b in range(NB):
+        for b in range(BANKS):
             nc.sync.dma_start(out=k_raw[:, 4 * b : 4 * b + 4, :], in_=k_view[:, 4 * b : 4 * b + 4, :])
         for j0, j1 in Q_REST:
             nc.sync.dma_start(out=q_raw[:, j0:j1, :], in_=q_view[:, j0:j1, :])
-        nc.sync.dma_start(out=v_raw[:].rearrange("p (a e) d -> p a (e d)", e=2), in_=v_view)
+        v_raw = const.tile([P, N], BF16)
+        nc.sync.dma_start(
+            out=v_raw[:].rearrange("p (a r) -> p a r", r=2 * P), in_=v.rearrange("(a p e) d -> p a (e d)", p=P, e=2)
+        )
 
-        qT = const.tile([P, N], BF16)
-        kT = const.tile([P, N], BF16)
+        q_t = const.tile([P, N], BF16)
+        k_t = const.tile([P, N], BF16)
         v_grouped = const.tile([P, N], BF16, align_bytes=64)
         v_codes = const.tile([P, N // 4], U32, align_bytes=64)
         v_scales = const.tile([P, N // 4], U8, align_bytes=64)
 
-        def regroup(dst, src):
-            for h in range(2):
-                nc.gpsimd.tensor_scalar(
-                    out=dst[:, 2048 * h : 2048 * h + 2048].rearrange("p (g c t) -> p g c t", g=4, t=4),
-                    in0=src[:, 2048 * h : 2048 * h + 2048].rearrange("p (g t c) -> p g c t", g=4, t=4),
-                    scalar1=1.0,
-                    scalar2=0.0,
-                    op0=ALU.mult,
-                    op1=ALU.add,
-                )
-
         def flip_input(raw, flipped, j0, j1):
-            tp = ps_t.tile([P, 8, P], BF16, name="tp_in", tag="tp")
+            bank = ps_flip.tile([P, 8, P], BF16, name="flip_in", tag="flip")
             for j in range(j0, j1):
-                nc.tensor.transpose(out=tp[:, j - j0, :], in_=raw[:, j, :], identity=ident[:])
+                nc.tensor.transpose(out=bank[:, j - j0, :], in_=raw[:, j, :], identity=ident[:])
             nc.scalar.copy(
-                out=flipped[:, j0 * P : j1 * P], in_=tp[:, 0 : j1 - j0, :].rearrange("p a b -> p (a b)")
+                out=flipped[:, j0 * P : j1 * P], in_=bank[:, 0 : j1 - j0, :].rearrange("p a b -> p (a b)")
             )
 
         live = {}
 
         def scores(i, b):
-            bd, sd = i // 4, i % 4
-            lo = sd * P
-            k0 = b * BANK
-            lq = qT[:, i * P : (i + 1) * P]
             if b == 0:
                 live["stash", i] = stash_pool.tile([P, N], F32, name="stash")
-                live["mparts", i] = small.tile([P, 16], F32, name="mparts")
-                live["n", i] = 0
-            stash = live["stash", i]
-            s_ps = ps_s.tile([P, BANK], F32, name="s_ps")
-            if b != bd:
-                nc.tensor.matmul(out=s_ps[:], lhsT=lq, rhs=kT[:, k0 : k0 + BANK], start=True, stop=True)
-            else:
-                if sd > 0:
-                    nc.tensor.matmul(out=s_ps[:, 0:lo], lhsT=lq, rhs=kT[:, k0 : k0 + lo], start=True, stop=True)
-                nc.tensor.matmul(
-                    out=s_ps[:, lo : lo + P], lhsT=lq, rhs=kT[:, k0 + lo : k0 + lo + P], start=True, stop=False
-                )
-                for j in range(3):
+                live["maxima", i] = small.tile([P, BANKS], F32, name="maxima")
+            diagonal_bank, diagonal_block = i // 4, i % 4
+            keys = slice(b * BANK, (b + 1) * BANK)
+            bank = ps_scores.tile([P, BANK], F32, name="bank")
+            nc.tensor.matmul(
+                out=bank[:], lhsT=q_t[:, i * P : (i + 1) * P], rhs=k_t[:, keys], start=True, stop=(b != diagonal_bank)
+            )
+            if b == diagonal_bank:
+                for block in range(diagonal_block, 4):
                     nc.tensor.matmul(
-                        out=s_ps[:, lo : lo + P], lhsT=ident[:], rhs=tri[j][:], start=False, stop=(j == 2)
+                        out=bank[:, block * P : (block + 1) * P],
+                        lhsT=(add_diagonal if block == diagonal_block else add_right)[:],
+                        rhs=ident_f[:],
+                        start=False,
+                        stop=(block == 3),
+                        is_transpose=True,
                     )
-                if sd < 3:
-                    nc.tensor.matmul(
-                        out=s_ps[:, lo + P : BANK], lhsT=lq, rhs=kT[:, k0 + lo + P : k0 + BANK], start=True, stop=True
-                    )
-            if b < bd:
-                parts = [(0, BANK, 0.0)]
-            elif b > bd:
-                parts = [(0, BANK, ROOT)]
-            else:
-                parts = [(0, lo + P, 0.0)]
-                if sd < 3:
-                    parts.append((lo + P, BANK, ROOT))
-            for c0, c1, shift in parts:
-                n_parts = live["n", i]
-                nc.vector.tensor_scalar(
-                    out=stash[:, k0 + c0 : k0 + c1],
-                    in0=s_ps[:, c0:c1],
-                    scalar1=shift,
-                    scalar2=None,
-                    op0=ALU.add,
-                    op1=ALU.max,
-                    accum_out=live["mparts", i][:, n_parts : n_parts + 1],
-                )
-                live["n", i] = n_parts + 1
+            nc.vector.tensor_scalar(
+                out=live["stash", i][:, keys],
+                in0=bank[:],
+                scalar1=(ROOT if b > diagonal_bank else 0.0),
+                scalar2=None,
+                op0=ALU.add,
+                op1=ALU.max,
+                accum_out=live["maxima", i][:, b : b + 1],
+            )
 
         def row_bias(i):
-            n_parts = live["n", i]
-            junk = small.tile([P, 16], F32, name="junk")
-            nbias = small.tile([P, 1], F32, name="nbias")
+            scaled = small.tile([P, BANKS], F32, name="scaled")
+            live["bias", i] = small.tile([P, 1], F32, name="bias")
             nc.vector.tensor_scalar(
-                out=junk[:, 0:n_parts],
-                in0=live["mparts", i][:, 0:n_parts],
-                scalar1=-SCALE,
+                out=scaled[:],
+                in0=live["maxima", i][:],
+                scalar1=-1.0 / ROOT,
                 scalar2=None,
                 op0=ALU.mult,
                 op1=ALU.min,
-                accum_out=nbias[:, 0:1],
+                accum_out=live["bias", i][:],
             )
-            live["nbias", i] = nbias
 
         def exponentials(i):
-            e_sb = e_pool.tile([P, N], BF16, name="e_sb")
-            rowsum = small.tile([P, 1], F32, name="rowsum")
+            live["e", i] = e_pool.tile([P, N], BF16, name="e")
+            live["rowsum", i] = small.tile([P, 1], F32, name="rowsum")
             nc.scalar.activation(
-                out=e_sb[:],
+                out=live["e", i][:],
                 in_=live["stash", i][:],
                 func=ACT.Exp,
-                bias=live["nbias", i][:, 0:1],
-                scale=SCALE,
-                accum_out=rowsum[:, 0:1],
+                bias=live["bias", i][:],
+                scale=1.0 / ROOT,
+                accum_out=live["rowsum", i][:],
             )
-            live["e", i] = e_sb
-            live["rowsum", i] = rowsum
 
         def flip_e(i, c):
             if c == 0:
                 live["grouped", i] = grouped_pool.tile([P, N], BF16, name="grouped", align_bytes=64)
-            tp = ps_t.tile([P, 4, P], F32, name="tp_e", tag="tp")
+            bank = ps_flip.tile([P, 4, P], F32, name="flip_e", tag="flip")
             words = live["e", i][:].bitcast(F32)
-            for w in range(4):
-                nc.tensor.transpose(
-                    out=tp[:, w, :], in_=words[:, (4 * c + w) * P : (4 * c + w + 1) * P], identity=ident_f[:]
-                )
-            copy = nc.vector.tensor_copy if i == NT - 2 else nc.scalar.copy
+            for w in range(4 * c, 4 * c + 4):
+                nc.tensor.transpose(out=bank[:, w - 4 * c, :], in_=words[:, w * P : (w + 1) * P], identity=ident_f[:])
+            copy = nc.vector.tensor_copy if i == TILES - 2 else nc.scalar.copy
             copy(
                 out=live["grouped", i][:]
-                .bitcast(F32)[:, 512 * c : 512 * c + 512]
-                .rearrange("p (g c u) -> p g c u", g=2, u=2),
-                in_=tp[:].rearrange("p (g u) c -> p g c u", u=2),
+                .bitcast(F32)[:, BANK * c : BANK * (c + 1)]
+                .rearrange("p (g q u) -> p g q u", g=2, u=2),
+                in_=bank[:].rearrange("p (g u) q -> p g q u", u=2),
             )
 
         def quantise_e(i):
-            codes = work.tile([P, N // 4], U32, name="codes", align_bytes=64)
-            scales = work.tile([P, N // 4], U8, name="scales", align_bytes=64)
-            nc.vector.quantize_mx(out=codes[:].bitcast(FP8X4), scales=scales[:], in_=live["grouped", i][:])
-            rinv = small.tile([P, 1], F32, name="rinv")
-            nc.vector.reciprocal(out=rinv[:, 0:1], in_=live["rowsum", i][:, 0:1])
-            live["codes", i] = codes
-            live["scales", i] = scales
-            live["rinv", i] = rinv
+            live["codes", i] = codes_pool.tile([P, N // 4], U32, name="codes", align_bytes=64)
+            live["scales", i] = codes_pool.tile([P, N // 4], U8, name="scales", align_bytes=64)
+            nc.vector.quantize_mx(
+                out=live["codes", i][:].bitcast(FP8X4), scales=live["scales", i][:], in_=live["grouped", i][:]
+            )
+            live["reciprocal", i] = small.tile([P, 1], F32, name="reciprocal")
+            nc.vector.reciprocal(out=live["reciprocal", i][:], in_=live["rowsum", i][:])
 
         def weighted_sum(i, g0, g1):
             if g0 == 0:
-                live["acc", i] = ps_o.tile([P, D], F32, name="acc")
+                live["sums", i] = ps_out.tile([P, P], F32, name="sums")
             for g in range(g0, g1):
                 cols = slice(g * P, (g + 1) * P)
                 nc.tensor.matmul_mx(
-                    out=live["acc", i][:],
+                    out=live["sums", i][:],
                     lhsT=live["codes", i][:, cols].bitcast(FP8X4),
                     lhsT_scale=live["scales", i][:, cols],
                     rhs=v_codes[:, cols].bitcast(FP8X4),
                     rhs_scale=v_scales[:, cols],
                     start=(g == 0),
-                    stop=(g == 7),
+                    stop=(g == BANKS - 1),
                 )
 
         def normalise(i):
-            o_sb = small.tile([P, D], F32, name="o_sb")
-            nc.scalar.activation(out=o_sb[:], in_=live["acc", i][:], func=ACT.Copy, scale=live["rinv", i][:, 0:1])
-            nc.sync.dma_start(out=out[i * P : (i + 1) * P, :], in_=o_sb[:])
+            result = small.tile([P, P], F32, name="result")
+            nc.scalar.activation(out=result[:], in_=live["sums", i][:], func=ACT.Copy, scale=live["reciprocal", i][:])
+            nc.sync.dma_start(out=out[i * P : (i + 1) * P, :], in_=result[:])
 
         def has(i):
-            return 0 <= i < NT
+            return 0 <= i < TILES
 
-        flip_input(q_raw, qT, 0, 1)
-        regroup(v_grouped, v_raw[:].rearrange("p j d -> p (j d)"))
-        for n in range(NT + 4):
+        flip_input(q_raw, q_t, 0, 1)
+        for h in range(2):
+            half = slice(h * N // 2, (h + 1) * N // 2)
+            nc.gpsimd.tensor_scalar(
+                out=v_grouped[:, half].rearrange("p (g c t) -> p g c t", g=4, t=4),
+                in0=v_raw[:, half].rearrange("p (g t c) -> p g c t", g=4, t=4),
+                scalar1=1.0,
+                scalar2=0.0,
+                op0=ALU.mult,
+                op1=ALU.add,
+            )
+
+        for n in range(TILES + 4):
             if has(n - 1):
                 exponentials(n - 1)
             if has(n - 4):
                 quantise_e(n - 4)
-            for b in range(NB):
+            for b in range(BANKS):
                 if n == 0:
-                    flip_input(k_raw, kT, 4 * b, 4 * b + 4)
+                    flip_input(k_raw, k_t, 4 * b, 4 * b + 4)
                 if n == 1 and b < 3:
-                    flip_input(q_raw, qT, Q_REST[b + 1][0], Q_REST[b + 1][1])
+                    flip_input(q_raw, q_t, Q_REST[b + 1][0], Q_REST[b + 1][1])
                 if has(n - 2) and 1 <= b <= 3:
                     flip_e(n - 2, b - 1)
                 if has(n - 4) and 4 <= b <= 6:
-                    weighted_sum(n - 4, 3 * (b - 4), min(3 * (b - 4) + 3, 8))
+                    weighted_sum(n - 4, 3 * (b - 4), min(3 * (b - 4) + 3, BANKS))
                 if has(n):
                     scores(n, b)
             if has(n - 4):
@@ -256,6 +226,6 @@ def tile_scaled_dot_product_kernel(tc, q, k, v, out):
             if has(n):
                 row_bias(n)
             if n == 0:
-                flip_input(q_raw, qT, Q_REST[0][0], Q_REST[0][1])
+                flip_input(q_raw, q_t, Q_REST[0][0], Q_REST[0][1])
             if n == 1:
                 nc.vector.quantize_mx(out=v_codes[:].bitcast(FP8X4), scales=v_scales[:], in_=v_grouped[:])

import math
from contextlib import ExitStack

import concourse.mybir as mybir
from concourse.masks import make_identity

F32 = mybir.dt.float32
BF16 = mybir.dt.bfloat16
U32 = mybir.dt.uint32
U8 = mybir.dt.uint8
FP8X4 = mybir.dt.float8_e4m3fn_x4
ALU = mybir.AluOpType
ACT = mybir.ActivationFunctionType

P = 128
N = 4096
TILES = N // P
BANK = 512
BANKS = N // BANK
FLOPS = 2 * N * N * (P + P)

ROOT = math.sqrt(128.0)
Q_REST = ((1, 8), (8, 16), (16, 24), (24, 32))


def tile_scaled_dot_product_kernel(tc, q, k, v, out):
    nc = tc.nc
    with ExitStack() as ctx:
        const = ctx.enter_context(tc.tile_pool(name="const", bufs=1))
        stash_pool = ctx.enter_context(tc.tile_pool(name="stash", bufs=3))
        e_pool = ctx.enter_context(tc.tile_pool(name="e", bufs=3))
        grouped_pool = ctx.enter_context(tc.tile_pool(name="grouped", bufs=3))
        codes_pool = ctx.enter_context(tc.tile_pool(name="codes", bufs=2))
        small = ctx.enter_context(tc.tile_pool(name="small", bufs=6))
        ps_scores = ctx.enter_context(tc.psum_pool(name="ps_scores", bufs=4))
        ps_flip = ctx.enter_context(tc.psum_pool(name="ps_flip", bufs=3))
        ps_out = ctx.enter_context(tc.psum_pool(name="ps_out", bufs=1))
        ctx.enter_context(tc.manual_schedule())

        ident = const.tile([P, P], BF16)
        make_identity(nc, ident[:])
        ident_f = const.tile([P, P], F32)
        make_identity(nc, ident_f[:])
        below = const.tile([P, P], F32)
        nc.gpsimd.memset(below[:], 0.0)
        nc.gpsimd.affine_select(
            out=below[:],
            in_=below[:],
            compare_op=ALU.is_ge,
            fill=1.0,
            base=0,
            pattern=[[1, P]],
            channel_multiplier=-1,
        )
        ones = const.tile([P, P], F32)
        nc.gpsimd.memset(ones[:], 1.0)
        add_diagonal = const.tile([P, P], F32)
        nc.vector.tensor_scalar(out=add_diagonal[:], in0=below[:], scalar1=ROOT, scalar2=None, op0=ALU.mult)
        add_right = const.tile([P, P], F32)
        nc.vector.tensor_scalar(out=add_right[:], in0=ones[:], scalar1=ROOT, scalar2=None, op0=ALU.mult)

        q_raw = const.tile([P, TILES, P], BF16)
        k_raw = const.tile([P, TILES, P], BF16)
        q_view = q.rearrange("(j p) d -> p j d", p=P)
        k_view = k.rearrange("(j p) d -> p j d", p=P)
        nc.sync.dma_start(out=q_raw[:, 0:1, :], in_=q_view[:, 0:1, :])
        for b in range(BANKS):
            nc.sync.dma_start(out=k_raw[:, 4 * b : 4 * b + 4, :], in_=k_view[:, 4 * b : 4 * b + 4, :])
        for j0, j1 in Q_REST:
            nc.sync.dma_start(out=q_raw[:, j0:j1, :], in_=q_view[:, j0:j1, :])
        v_raw = const.tile([P, N], BF16)
        nc.sync.dma_start(
            out=v_raw[:].rearrange("p (a r) -> p a r", r=2 * P), in_=v.rearrange("(a p e) d -> p a (e d)", p=P, e=2)
        )

        q_t = const.tile([P, N], BF16)
        k_t = const.tile([P, N], BF16)
        v_grouped = const.tile([P, N], BF16, align_bytes=64)
        v_codes = const.tile([P, N // 4], U32, align_bytes=64)
        v_scales = const.tile([P, N // 4], U8, align_bytes=64)

        def flip_input(raw, flipped, j0, j1):
            bank = ps_flip.tile([P, 8, P], BF16, name="flip_in", tag="flip")
            for j in range(j0, j1):
                nc.tensor.transpose(out=bank[:, j - j0, :], in_=raw[:, j, :], identity=ident[:])
            nc.scalar.copy(
                out=flipped[:, j0 * P : j1 * P], in_=bank[:, 0 : j1 - j0, :].rearrange("p a b -> p (a b)")
            )

        live = {}

        def scores(i, b):
            if b == 0:
                live["stash", i] = stash_pool.tile([P, N], F32, name="stash")
                live["maxima", i] = small.tile([P, BANKS], F32, name="maxima")
            diagonal_bank, diagonal_block = i // 4, i % 4
            keys = slice(b * BANK, (b + 1) * BANK)
            bank = ps_scores.tile([P, BANK], F32, name="bank")
            nc.tensor.matmul(
                out=bank[:], lhsT=q_t[:, i * P : (i + 1) * P], rhs=k_t[:, keys], start=True, stop=(b != diagonal_bank)
            )
            if b == diagonal_bank:
                for block in range(diagonal_block, 4):
                    nc.tensor.matmul(
                        out=bank[:, block * P : (block + 1) * P],
                        lhsT=(add_diagonal if block == diagonal_block else add_right)[:],
                        rhs=ident_f[:],
                        start=False,
                        stop=(block == 3),
                        is_transpose=True,
                    )
            nc.vector.tensor_scalar(
                out=live["stash", i][:, keys],
                in0=bank[:],
                scalar1=(ROOT if b > diagonal_bank else 0.0),
                scalar2=None,
                op0=ALU.add,
                op1=ALU.max,
                accum_out=live["maxima", i][:, b : b + 1],
            )

        def row_bias(i):
            scaled = small.tile([P, BANKS], F32, name="scaled")
            live["bias", i] = small.tile([P, 1], F32, name="bias")
            nc.vector.tensor_scalar(
                out=scaled[:],
                in0=live["maxima", i][:],
                scalar1=-1.0 / ROOT,
                scalar2=None,
                op0=ALU.mult,
                op1=ALU.min,
                accum_out=live["bias", i][:],
            )

        def exponentials(i):
            live["e", i] = e_pool.tile([P, N], BF16, name="e")
            live["rowsum", i] = small.tile([P, 1], F32, name="rowsum")
            nc.scalar.activation(
                out=live["e", i][:],
                in_=live["stash", i][:],
                func=ACT.Exp,
                bias=live["bias", i][:],
                scale=1.0 / ROOT,
                accum_out=live["rowsum", i][:],
            )

        def flip_e(i, c):
            if c == 0:
                live["grouped", i] = grouped_pool.tile([P, N], BF16, name="grouped", align_bytes=64)
            bank = ps_flip.tile([P, 4, P], F32, name="flip_e", tag="flip")
            words = live["e", i][:].bitcast(F32)
            for w in range(4 * c, 4 * c + 4):
                nc.tensor.transpose(out=bank[:, w - 4 * c, :], in_=words[:, w * P : (w + 1) * P], identity=ident_f[:])
            copy = nc.vector.tensor_copy if i == TILES - 2 else nc.scalar.copy
            copy(
                out=live["grouped", i][:]
                .bitcast(F32)[:, BANK * c : BANK * (c + 1)]
                .rearrange("p (g q u) -> p g q u", g=2, u=2),
                in_=bank[:].rearrange("p (g u) q -> p g q u", u=2),
            )

        def quantise_e(i):
            live["codes", i] = codes_pool.tile([P, N // 4], U32, name="codes", align_bytes=64)
            live["scales", i] = codes_pool.tile([P, N // 4], U8, name="scales", align_bytes=64)
            nc.vector.quantize_mx(
                out=live["codes", i][:].bitcast(FP8X4), scales=live["scales", i][:], in_=live["grouped", i][:]
            )
            live["reciprocal", i] = small.tile([P, 1], F32, name="reciprocal")
            nc.vector.reciprocal(out=live["reciprocal", i][:], in_=live["rowsum", i][:])

        def weighted_sum(i, g0, g1):
            if g0 == 0:
                live["sums", i] = ps_out.tile([P, P], F32, name="sums")
            for g in range(g0, g1):
                cols = slice(g * P, (g + 1) * P)
                nc.tensor.matmul_mx(
                    out=live["sums", i][:],
                    lhsT=live["codes", i][:, cols].bitcast(FP8X4),
                    lhsT_scale=live["scales", i][:, cols],
                    rhs=v_codes[:, cols].bitcast(FP8X4),
                    rhs_scale=v_scales[:, cols],
                    start=(g == 0),
                    stop=(g == BANKS - 1),
                )

        def normalise(i):
            result = small.tile([P, P], F32, name="result")
            nc.scalar.activation(out=result[:], in_=live["sums", i][:], func=ACT.Copy, scale=live["reciprocal", i][:])
            nc.sync.dma_start(out=out[i * P : (i + 1) * P, :], in_=result[:])

        def has(i):
            return 0 <= i < TILES

        flip_input(q_raw, q_t, 0, 1)
        for h in range(2):
            half = slice(h * N // 2, (h + 1) * N // 2)
            nc.gpsimd.tensor_scalar(
                out=v_grouped[:, half].rearrange("p (g c t) -> p g c t", g=4, t=4),
                in0=v_raw[:, half].rearrange("p (g t c) -> p g c t", g=4, t=4),
                scalar1=1.0,
                scalar2=0.0,
                op0=ALU.mult,
                op1=ALU.add,
            )

        for n in range(TILES + 4):
            if has(n - 1):
                exponentials(n - 1)
            if has(n - 4):
                quantise_e(n - 4)
            for b in range(BANKS):
                if n == 0:
                    flip_input(k_raw, k_t, 4 * b, 4 * b + 4)
                if n == 1 and b < 3:
                    flip_input(q_raw, q_t, Q_REST[b + 1][0], Q_REST[b + 1][1])
                if has(n - 2) and 1 <= b <= 3:
                    flip_e(n - 2, b - 1)
                if has(n - 4) and 4 <= b <= 6:
                    weighted_sum(n - 4, 3 * (b - 4), min(3 * (b - 4) + 3, BANKS))
                if has(n):
                    scores(n, b)
            if has(n - 4):
                normalise(n - 4)
            if has(n - 2):
                flip_e(n - 2, 3)
            if has(n):
                row_bias(n)
            if n == 0:
                flip_input(q_raw, q_t, Q_REST[0][0], Q_REST[0][1])
            if n == 1:
                nc.vector.quantize_mx(out=v_codes[:].bitcast(FP8X4), scales=v_scales[:], in_=v_grouped[:])
